import numpy as np
import ml_dtypes


def mxq(x, axis, fmt="e4m3"):
    dtype, down = {"e4m3": (ml_dtypes.float8_e4m3fn, 7), "e5m2": (ml_dtypes.float8_e5m2, 14)}[fmt]
    v = np.moveaxis(np.asarray(x, np.float32).astype(ml_dtypes.bfloat16).astype(np.float64), axis, -1)
    blocks = v.reshape(v.shape[:-1] + (-1, 32))
    amax = np.abs(blocks).max(-1, keepdims=True)
    byte = np.maximum(np.where(amax > 0, np.frexp(amax)[1] - 1 + 127, 0) - down, 1)
    scale = np.exp2(byte - 127.0)
    codes = (blocks / scale).astype(np.float32).astype(dtype).astype(np.float64)
    return np.moveaxis((codes * scale).reshape(v.shape), -1, axis)


WIDE = False


def mx_kscale(k):
    if not WIDE:
        return np.ones(k)
    levels = np.array([10, -10, 5, -5, 0])
    a = np.random.permutation(np.resize(levels, k // 512 * 4)).reshape(k // 512, 4)
    idx = np.arange(k)
    return np.exp2(a[idx // 512, idx % 128 // 32])


BF16 = ml_dtypes.bfloat16


def bf(x):
    return np.asarray(x, np.float32).astype(BF16)


def f64(x):
    return np.asarray(x).astype(np.float64)


N, DIN, H1, H2, C, NC, G = 1024, 512, 512, 256, 128, 512, 8


def setup_inputs():
    s = mx_kscale(N)
    centres = np.random.standard_normal((G, C)) * 1.5
    z = centres[np.random.randint(G, size=N)] + 0.5 * np.random.standard_normal((N, C))
    return {"feats": bf(1.0 / (1.0 + np.exp(-z))),
            "pf_offdiag": bf(np.random.uniform(size=(N, N)) / np.sqrt(N) * (1.0 - np.eye(N)) * s),
            "members": bf((np.random.uniform(size=(N, NC)) < 0.1) * (0.5 + np.random.uniform(size=(N, NC))) / s[:, None])}


def reference(feats, pf_offdiag, members):
    sq = np.sum(f64(feats) * f64(feats), axis=-1)
    d2 = sq[:, None] + sq[None, :] - 2.0 * (f64(feats) @ f64(feats).T)
    dist = np.sqrt(np.maximum(d2, 1e-12))
    force = dist * f64(pf_offdiag)
    return mxq(force, 1, "e4m3") @ mxq(f64(members), 0, "e4m3")

@@ -1,0 +1,249 @@
+from contextlib import ExitStack
+
+import concourse.mybir as mybir
+from concourse.masks import make_identity
+
+F32 = mybir.dt.float32
+BF16 = mybir.dt.bfloat16
+U32 = mybir.dt.uint32
+U8 = mybir.dt.uint8
+FP8X4 = mybir.dt.float8_e4m3fn_x4
+ALU = mybir.AluOpType
+ACT = mybir.ActivationFunctionType
+
+NODES = 1024
+CODE = 128
+CLUSTERS = 512
+
+P = 128
+PACK = 4
+K_PASS = P * PACK
+PASSES = NODES // K_PASS
+TILES = NODES // P
+BANK = 512
+
+GROUP_TILES = 2
+GROUP = GROUP_TILES * P
+GROUPS = NODES // GROUP
+STEPS = GROUPS * PASSES
+PAIR = 2
+WORDS = PACK // PAIR
+
+LAG = 2
+
+FLOPS = 2 * NODES * NODES * CODE + 2 * NODES * NODES * CLUSTERS
+
+
+def tile_controencodnet_pb_kernel(tc, feats, pf_offdiag, members, out):
+    nc = tc.nc
+
+    feats_nodes = feats.rearrange("(g p t) c -> p g t c", g=PASSES, t=PACK)
+    pf_rows = pf_offdiag.rearrange("(g p t) j -> p g t j", g=PASSES, t=PACK)
+    members_nodes = members.rearrange("(g p t) c -> p g t c", g=PASSES, t=PACK)
+    out_rows = out.rearrange("(g p t) c -> p g t c", g=PASSES, t=PACK)
+
+    with ExitStack() as ctx:
+        ctx.enter_context(tc.manual_schedule())
+        keep = ctx.enter_context(tc.tile_pool(name="keep", bufs=1))
+        work = ctx.enter_context(tc.tile_pool(name="work", bufs=LAG + 1))
+        gram_psum = ctx.enter_context(tc.psum_pool(name="gram_psum", bufs=4))
+        pft_psum = ctx.enter_context(tc.psum_pool(name="pft_psum", bufs=2))
+        acc_psum = ctx.enter_context(tc.psum_pool(name="acc_psum", bufs=GROUP_TILES))
+
+        feats_sb = keep.tile([P, PASSES, PACK, CODE], BF16)
+        nc.sync.dma_start(out=feats_sb[:], in_=feats_nodes)
+        members_sb = keep.tile([P, PASSES, PACK, CLUSTERS], BF16)
+        for g in range(PASSES):
+            nc.sync.dma_start(out=members_sb[:, g], in_=members_nodes[:, g])
+        pf_sb = []
+        for q in range(GROUPS):
+            g_row, t_row = divmod(q * GROUP_TILES, PACK)
+            pf_group = keep.tile([P, GROUP_TILES, NODES], BF16, name="pf_group%d" % q)
+            nc.sync.dma_start(
+                out=pf_group[:], in_=pf_rows[:, g_row, t_row : t_row + GROUP_TILES, :]
+            )
+            pf_sb.append(pf_group)
+
+        one = keep.tile([P, 1], F32)
+        nc.vector.memset(one[:], 1.0)
+        nc.scalar.activation(out=one[:], in_=one[:], func=ACT.Sqrt)
+        ident_bf16 = keep.tile([P, P], BF16)
+        make_identity(nc, ident_bf16[:])
+        ident_f32 = keep.tile([P, P], F32)
+        make_identity(nc, ident_f32[:])
+
+        featsT_ps = pft_psum.tile([P, NODES], BF16, tag="pft")
+        for a in range(TILES):
+            g, t = divmod(a, PACK)
+            nc.tensor.transpose(
+                featsT_ps[:, a * P : (a + 1) * P], feats_sb[:, g, t, :], ident_bf16[:]
+            )
+        featsT = keep.tile([P, NODES], BF16)
+        nc.vector.tensor_copy(out=featsT[:], in_=featsT_ps[:])
+
+        def gram(s):
+            q, g = divmod(s, PASSES)
+            banks = []
+            for b in range(PACK * GROUP // BANK):
+                bank = gram_psum.tile([P, BANK // GROUP, GROUP], F32, tag="gram", name="gram_bank")
+                for h in range(BANK // GROUP):
+                    a = g * PACK + b * (BANK // GROUP) + h
+                    nc.tensor.matmul(
+                        out=bank[:, h, :],
+                        lhsT=featsT[:, a * P : (a + 1) * P],
+                        rhs=featsT[:, q * GROUP : (q + 1) * GROUP],
+                        start=True,
+                        stop=True,
+                    )
+                banks.append(bank)
+            return banks
+
+        gram_banks = {0: gram(0)}
+
+        squares = keep.tile([P, TILES, CODE], F32)
+        sq = keep.tile([P, TILES], F32)
+        for a in range(TILES):
+            g, t = divmod(a, PACK)
+            nc.scalar.activation(
+                out=squares[:, a, :],
+                in_=feats_sb[:, g, t, :],
+                func=ACT.Square,
+                accum_out=sq[:, a : a + 1],
+            )
+        neg_half_sq = keep.tile([P, TILES], F32)
+        nc.vector.tensor_scalar_mul(out=neg_half_sq[:], in0=sq[:], scalar1=-0.5)
+        neg_half_sq_row = keep.tile([P, NODES], F32)
+        for half in range(NODES // BANK):
+            row_ps = acc_psum.tile([P, BANK], F32, tag="acc")
+            for k in range(BANK // P):
+                a = half * (BANK // P) + k
+                nc.tensor.transpose(
+                    row_ps[:, k * P : (k + 1) * P],
+                    neg_half_sq[:, a : a + 1].to_broadcast([P, P]),
+                    ident_f32[:],
+                )
+            row_sb = neg_half_sq_row[:, half * BANK : (half + 1) * BANK]
+            if half == 0:
+                nc.scalar.copy(out=row_sb, in_=row_ps[:])
+            else:
+                nc.vector.tensor_copy(out=row_sb, in_=row_ps[:])
+
+        members_grouped = keep.tile([P, PASSES, CLUSTERS, PACK], BF16, align_bytes=64)
+        nc.scalar.copy(
+            out=members_grouped[:, 0], in_=members_sb[:, 0].rearrange("p t c -> p c t")
+        )
+        nc.gpsimd.tensor_scalar(
+            out=members_grouped[:, 1],
+            in0=members_sb[:, 1].rearrange("p t c -> p c t"),
+            scalar1=1.0,
+            scalar2=0.0,
+            op0=ALU.mult,
+            op1=ALU.add,
+        )
+        members_codes = keep.tile([P, PASSES, CLUSTERS], U32, align_bytes=64)
+        members_scales = keep.tile([P, PASSES, CLUSTERS], U8, align_bytes=64)
+
+        def quantise_members():
+            for g in range(PASSES):
+                nc.vector.quantize_mx(
+                    out=members_codes[:, g, :].bitcast(FP8X4),
+                    scales=members_scales[:, g, :],
+                    in_=members_grouped[:, g].rearrange("p c t -> p (c t)"),
+                )
+
+        def distances(s, banks):
+            q, g = divmod(s, PASSES)
+            neg_half_d2 = work.tile([P, PACK, GROUP], F32, tag="neg_half_d2")
+            for t in range(PACK):
+                b, h = divmod(t, BANK // GROUP)
+                a = g * PACK + t
+                nc.vector.scalar_tensor_tensor(
+                    out=neg_half_d2[:, t, :],
+                    in0=banks[b][:, h, :],
+                    scalar=neg_half_sq[:, a : a + 1],
+                    in1=neg_half_sq_row[:, q * GROUP : (q + 1) * GROUP],
+                    op0=ALU.add,
+                    op1=ALU.add,
+                )
+            dist = work.tile([P, GROUP, PACK], F32, tag="dist")
+            nc.gpsimd.tensor_scalar(
+                out=dist[:],
+                in0=neg_half_d2[:].rearrange("p t n -> p n t"),
+                scalar1=-2.0,
+                scalar2=1e-12,
+                op0=ALU.mult,
+                op1=ALU.max,
+            )
+            nc.scalar.activation(out=dist[:], in_=dist[:], func=ACT.Sqrt)
+            return dist
+
+        def transpose_pf(s):
+            q, g = divmod(s, PASSES)
+            pfT = pft_psum.tile([P, WORDS * GROUP], F32, tag="pft")
+            for r in range(GROUP_TILES):
+                row_words = pf_sb[q][:, r, :].bitcast(F32)
+                pass_words = K_PASS // PAIR
+                for w in range(WORDS):
+                    nc.tensor.transpose(
+                        pfT[:, w * GROUP + r * P : w * GROUP + (r + 1) * P],
+                        row_words[:, g * pass_words + w : (g + 1) * pass_words : WORDS],
+                        ident_f32[:],
+                    )
+            return pfT
+
+        def multiply(dist, pfT):
+            force = work.tile([P, GROUP * PACK], BF16, tag="force", align_bytes=64)
+            nc.vector.tensor_tensor(
+                out=force[:].rearrange("p (n w e) -> p n w e", w=WORDS, e=PAIR),
+                in0=dist[:].rearrange("p n (w e) -> p n w e", e=PAIR),
+                in1=pfT[:].bitcast(BF16).rearrange("p (w n e) -> p n w e", w=WORDS, e=PAIR),
+                op=ALU.mult,
+            )
+            return force
+
+        def quantise(force):
+            codes = work.tile([P, GROUP], U32, tag="codes", align_bytes=64)
+            scales = work.tile([P, GROUP], U8, tag="scales", align_bytes=64)
+            nc.vector.quantize_mx(out=codes[:].bitcast(FP8X4), scales=scales[:], in_=force[:])
+            return codes, scales
+
+        def multiply_members(s, codes, scales, acc):
+            q, g = divmod(s, PASSES)
+            for r in range(GROUP_TILES):
+                if g == 0:
+                    acc[r] = acc_psum.tile([P, CLUSTERS], F32, tag="acc", name="acc_bank")
+                nc.tensor.matmul_mx(
+                    out=acc[r][:],
+                    lhsT=codes[:, r * P : (r + 1) * P].bitcast(FP8X4),
+                    lhsT_scale=scales[:, r * P : (r + 1) * P],
+                    rhs=members_codes[:, g, :].bitcast(FP8X4),
+                    rhs_scale=members_scales[:, g, :],
+                    start=(g == 0),
+                    stop=(g == PASSES - 1),
+                )
+            if g == PASSES - 1:
+                for r in range(GROUP_TILES):
+                    g_row, t_row = divmod(q * GROUP_TILES + r, PACK)
+                    result = work.tile([P, CLUSTERS], F32, tag="result")
+                    nc.scalar.copy(out=result[:], in_=acc[r][:])
+                    nc.sync.dma_start(out=out_rows[:, g_row, t_row, :], in_=result[:])
+
+        dists = {}
+        pfTs = {}
+        acc = {}
+        for s in range(STEPS + LAG):
+            done = s - LAG
+            if done == 0:
+                quantise_members()
+            if done >= 0:
+                force = multiply(dists[done], pfTs[done])
+            if s + 1 < STEPS:
+                gram_banks[s + 1] = gram(s + 1)
+            if s < STEPS:
+                dists[s] = distances(s, gram_banks[s])
+            if done >= 0:
+                codes, scales = quantise(force)
+            if s < STEPS:
+                pfTs[s] = transpose_pf(s)
+            if done >= 0:
+                multiply_members(done, codes, scales, acc)

@@ -14,6 +14,7 @@ ACT = mybir.ActivationFunctionType
 NODES = 1024
 CODE = 128
 CLUSTERS = 512
+D2_FLOOR = 1e-12
 
 P = 128
 PACK = 4
@@ -151,7 +152,7 @@ def tile_controencodnet_pb_kernel(tc, feats, pf_offdiag, members, out):
                     in_=members_grouped[:, g].rearrange("p c t -> p (c t)"),
                 )
 
-        def distances(s, banks):
+        def add_norms(s, banks):
             q, g = divmod(s, PASSES)
             neg_half_d2 = work.tile([P, PACK, GROUP], F32, tag="neg_half_d2")
             for t in range(PACK):
@@ -165,16 +166,19 @@ def tile_controencodnet_pb_kernel(tc, feats, pf_offdiag, members, out):
                     op0=ALU.add,
                     op1=ALU.add,
                 )
-            dist = work.tile([P, GROUP, PACK], F32, tag="dist")
-            nc.gpsimd.tensor_scalar(
-                out=dist[:],
-                in0=neg_half_d2[:].rearrange("p t n -> p n t"),
-                scalar1=-2.0,
-                scalar2=1e-12,
-                op0=ALU.mult,
-                op1=ALU.max,
+            return neg_half_d2
+
+        def clamp_and_root(neg_half_d2):
+            nc.vector.tensor_scalar_min(
+                out=neg_half_d2[:], in0=neg_half_d2[:], scalar1=-0.5 * D2_FLOOR
             )
-            nc.scalar.activation(out=dist[:], in_=dist[:], func=ACT.Sqrt)
+            dist = work.tile([P, GROUP, PACK], F32, tag="dist")
+            nc.scalar.activation(
+                out=dist[:],
+                in_=neg_half_d2[:].rearrange("p t n -> p n t"),
+                func=ACT.Sqrt,
+                scale=-2.0,
+            )
             return dist
 
         def transpose_pf(s):
@@ -240,10 +244,11 @@ def tile_controencodnet_pb_kernel(tc, feats, pf_offdiag, members, out):
             if s + 1 < STEPS:
                 gram_banks[s + 1] = gram(s + 1)
             if s < STEPS:
-                dists[s] = distances(s, gram_banks[s])
+                neg_half_d2 = add_norms(s, gram_banks[s])
             if done >= 0:
                 codes, scales = quantise(force)
             if s < STEPS:
+                dists[s] = clamp_and_root(neg_half_d2)
                 pfTs[s] = transpose_pf(s)
             if done >= 0:
                 multiply_members(done, codes, scales, acc)

@@ -94,12 +94,20 @@ def tile_controencodnet_pb_kernel(tc, feats, pf_offdiag, members, out):
                         lhsT=featsT[:, a * P : (a + 1) * P],
                         rhs=featsT[:, q * GROUP : (q + 1) * GROUP],
                         start=True,
-                        stop=True,
+                        stop=False,
                     )
+                    for r in range(GROUP_TILES):
+                        row_tile = q * GROUP_TILES + r
+                        nc.tensor.matmul(
+                            out=bank[:, h, r * P : (r + 1) * P],
+                            lhsT=neg_half_sq[:, row_tile : row_tile + 1].to_broadcast([P, P]),
+                            rhs=ident_f32[:],
+                            is_transpose=True,
+                            start=False,
+                            stop=(r == GROUP_TILES - 1),
+                        )
                 banks.append(bank)
             return banks
-
-        gram_banks = {0: gram(0)}
 
         squares = keep.tile([P, TILES, CODE], F32)
         sq = keep.tile([P, TILES], F32)
@@ -113,21 +121,8 @@ def tile_controencodnet_pb_kernel(tc, feats, pf_offdiag, members, out):
             )
         neg_half_sq = keep.tile([P, TILES], F32)
         nc.vector.tensor_scalar_mul(out=neg_half_sq[:], in0=sq[:], scalar1=-0.5)
-        neg_half_sq_row = keep.tile([P, NODES], F32)
-        for half in range(NODES // BANK):
-            row_ps = acc_psum.tile([P, BANK], F32, tag="acc")
-            for k in range(BANK // P):
-                a = half * (BANK // P) + k
-                nc.tensor.transpose(
-                    row_ps[:, k * P : (k + 1) * P],
-                    neg_half_sq[:, a : a + 1].to_broadcast([P, P]),
-                    ident_f32[:],
-                )
-            row_sb = neg_half_sq_row[:, half * BANK : (half + 1) * BANK]
-            if half == 0:
-                nc.scalar.copy(out=row_sb, in_=row_ps[:])
-            else:
-                nc.vector.tensor_copy(out=row_sb, in_=row_ps[:])
+
+        gram_banks = {0: gram(0)}
 
         members_grouped = keep.tile([P, PASSES, CLUSTERS, PACK], BF16, align_bytes=64)
         nc.scalar.copy(
@@ -158,20 +153,17 @@ def tile_controencodnet_pb_kernel(tc, feats, pf_offdiag, members, out):
             for t in range(PACK):
                 b, h = divmod(t, BANK // GROUP)
                 a = g * PACK + t
-                nc.vector.scalar_tensor_tensor(
+                nc.vector.tensor_scalar(
                     out=neg_half_d2[:, t, :],
                     in0=banks[b][:, h, :],
-                    scalar=neg_half_sq[:, a : a + 1],
-                    in1=neg_half_sq_row[:, q * GROUP : (q + 1) * GROUP],
+                    scalar1=neg_half_sq[:, a : a + 1],
+                    scalar2=-0.5 * D2_FLOOR,
                     op0=ALU.add,
-                    op1=ALU.add,
+                    op1=ALU.min,
                 )
             return neg_half_d2
 
         def clamp_and_root(neg_half_d2):
-            nc.vector.tensor_scalar_min(
-                out=neg_half_d2[:], in0=neg_half_d2[:], scalar1=-0.5 * D2_FLOOR
-            )
             dist = work.tile([P, GROUP, PACK], F32, tag="dist")
             nc.scalar.activation(
                 out=dist[:],

@@ -27,6 +27,7 @@ GROUP_TILES = 2
 GROUP = GROUP_TILES * P
 GROUPS = NODES // GROUP
 STEPS = GROUPS * PASSES
+BANK_TILES = BANK // GROUP
 PAIR = 2
 WORDS = PACK // PAIR
 
@@ -52,7 +53,8 @@ def tile_controencodnet_pb_kernel(tc, feats, pf_offdiag, members, out):
         acc_psum = ctx.enter_context(tc.psum_pool(name="acc_psum", bufs=GROUP_TILES))
 
         feats_sb = keep.tile([P, PASSES, PACK, CODE], BF16)
-        nc.sync.dma_start(out=feats_sb[:], in_=feats_nodes)
+        for g in range(PASSES):
+            nc.sync.dma_start(out=feats_sb[:, g], in_=feats_nodes[:, g])
         members_sb = keep.tile([P, PASSES, PACK, CLUSTERS], BF16)
         for g in range(PASSES):
             nc.sync.dma_start(out=members_sb[:, g], in_=members_nodes[:, g])
@@ -73,41 +75,17 @@ def tile_controencodnet_pb_kernel(tc, feats, pf_offdiag, members, out):
         ident_f32 = keep.tile([P, P], F32)
         make_identity(nc, ident_f32[:])
 
-        featsT_ps = pft_psum.tile([P, NODES], BF16, tag="pft")
-        for a in range(TILES):
-            g, t = divmod(a, PACK)
-            nc.tensor.transpose(
-                featsT_ps[:, a * P : (a + 1) * P], feats_sb[:, g, t, :], ident_bf16[:]
-            )
         featsT = keep.tile([P, NODES], BF16)
-        nc.vector.tensor_copy(out=featsT[:], in_=featsT_ps[:])
-
-        def gram(s):
-            q, g = divmod(s, PASSES)
-            banks = []
-            for b in range(PACK * GROUP // BANK):
-                bank = gram_psum.tile([P, BANK // GROUP, GROUP], F32, tag="gram", name="gram_bank")
-                for h in range(BANK // GROUP):
-                    a = g * PACK + b * (BANK // GROUP) + h
-                    nc.tensor.matmul(
-                        out=bank[:, h, :],
-                        lhsT=featsT[:, a * P : (a + 1) * P],
-                        rhs=featsT[:, q * GROUP : (q + 1) * GROUP],
-                        start=True,
-                        stop=False,
-                    )
-                    for r in range(GROUP_TILES):
-                        row_tile = q * GROUP_TILES + r
-                        nc.tensor.matmul(
-                            out=bank[:, h, r * P : (r + 1) * P],
-                            lhsT=neg_half_sq[:, row_tile : row_tile + 1].to_broadcast([P, P]),
-                            rhs=ident_f32[:],
-                            is_transpose=True,
-                            start=False,
-                            stop=(r == GROUP_TILES - 1),
-                        )
-                banks.append(bank)
-            return banks
+        featsT_m2 = keep.tile([P, NODES], BF16)
+        for g in range(PASSES):
+            featsT_ps = pft_psum.tile([P, K_PASS], BF16, tag="pft")
+            for t in range(PACK):
+                nc.tensor.transpose(
+                    featsT_ps[:, t * P : (t + 1) * P], feats_sb[:, g, t, :], ident_bf16[:]
+                )
+            pass_cols = slice(g * K_PASS, (g + 1) * K_PASS)
+            nc.vector.tensor_copy(out=featsT[:, pass_cols], in_=featsT_ps[:])
+            nc.vector.tensor_scalar_mul(out=featsT_m2[:, pass_cols], in0=featsT_ps[:], scalar1=-2.0)
 
         squares = keep.tile([P, TILES, CODE], F32)
         sq = keep.tile([P, TILES], F32)
@@ -119,57 +97,71 @@ def tile_controencodnet_pb_kernel(tc, feats, pf_offdiag, members, out):
                 func=ACT.Square,
                 accum_out=sq[:, a : a + 1],
             )
-        neg_half_sq = keep.tile([P, TILES], F32)
-        nc.vector.tensor_scalar_mul(out=neg_half_sq[:], in0=sq[:], scalar1=-0.5)
-
-        gram_banks = {0: gram(0)}
 
         members_grouped = keep.tile([P, PASSES, CLUSTERS, PACK], BF16, align_bytes=64)
-        nc.scalar.copy(
-            out=members_grouped[:, 0], in_=members_sb[:, 0].rearrange("p t c -> p c t")
-        )
-        nc.gpsimd.tensor_scalar(
-            out=members_grouped[:, 1],
-            in0=members_sb[:, 1].rearrange("p t c -> p c t"),
-            scalar1=1.0,
-            scalar2=0.0,
-            op0=ALU.mult,
-            op1=ALU.add,
-        )
+        for g in range(PASSES):
+            nc.gpsimd.tensor_scalar(
+                out=members_grouped[:, g],
+                in0=members_sb[:, g].rearrange("p t c -> p c t"),
+                scalar1=1.0,
+                scalar2=0.0,
+                op0=ALU.mult,
+                op1=ALU.add,
+            )
         members_codes = keep.tile([P, PASSES, CLUSTERS], U32, align_bytes=64)
         members_scales = keep.tile([P, PASSES, CLUSTERS], U8, align_bytes=64)
 
-        def quantise_members():
-            for g in range(PASSES):
-                nc.vector.quantize_mx(
-                    out=members_codes[:, g, :].bitcast(FP8X4),
-                    scales=members_scales[:, g, :],
-                    in_=members_grouped[:, g].rearrange("p c t -> p (c t)"),
-                )
+        def quantise_members(g):
+            nc.vector.quantize_mx(
+                out=members_codes[:, g, :].bitcast(FP8X4),
+                scales=members_scales[:, g, :],
+                in_=members_grouped[:, g].rearrange("p c t -> p (c t)"),
+            )
 
-        def add_norms(s, banks):
+        def gram(s):
             q, g = divmod(s, PASSES)
-            neg_half_d2 = work.tile([P, PACK, GROUP], F32, tag="neg_half_d2")
+            banks = []
+            for b in range(PACK // BANK_TILES):
+                bank = gram_psum.tile([P, BANK_TILES, GROUP], F32, tag="gram", name="gram_bank")
+                for h in range(BANK_TILES):
+                    a = g * PACK + b * BANK_TILES + h
+                    nc.tensor.matmul(
+                        out=bank[:, h, :],
+                        lhsT=featsT_m2[:, a * P : (a + 1) * P],
+                        rhs=featsT[:, q * GROUP : (q + 1) * GROUP],
+                        start=True,
+                        stop=False,
+                    )
+                    for r in range(GROUP_TILES):
+                        row_tile = q * GROUP_TILES + r
+                        nc.tensor.matmul(
+                            out=bank[:, h, r * P : (r + 1) * P],
+                            lhsT=sq[:, row_tile : row_tile + 1].to_broadcast([P, P]),
+                            rhs=ident_f32[:],
+                            is_transpose=True,
+                            start=False,
+                            stop=(r == GROUP_TILES - 1),
+                        )
+                banks.append(bank)
+            return banks
+
+        def clamp_and_root(s, banks):
+            g = s % PASSES
+            d2 = work.tile([P, PACK, GROUP], F32, tag="d2")
             for t in range(PACK):
-                b, h = divmod(t, BANK // GROUP)
+                b, h = divmod(t, BANK_TILES)
                 a = g * PACK + t
                 nc.vector.tensor_scalar(
-                    out=neg_half_d2[:, t, :],
+                    out=d2[:, t, :],
                     in0=banks[b][:, h, :],
-                    scalar1=neg_half_sq[:, a : a + 1],
-                    scalar2=-0.5 * D2_FLOOR,
+                    scalar1=sq[:, a : a + 1],
+                    scalar2=D2_FLOOR,
                     op0=ALU.add,
-                    op1=ALU.min,
+                    op1=ALU.max,
                 )
-            return neg_half_d2
-
-        def clamp_and_root(neg_half_d2):
             dist = work.tile([P, GROUP, PACK], F32, tag="dist")
             nc.scalar.activation(
-                out=dist[:],
-                in_=neg_half_d2[:].rearrange("p t n -> p n t"),
-                func=ACT.Sqrt,
-                scale=-2.0,
+                out=dist[:], in_=d2[:].rearrange("p t n -> p n t"), func=ACT.Sqrt
             )
             return dist
 
@@ -224,23 +216,23 @@ def tile_controencodnet_pb_kernel(tc, feats, pf_offdiag, members, out):
                     nc.scalar.copy(out=result[:], in_=acc[r][:])
                     nc.sync.dma_start(out=out_rows[:, g_row, t_row, :], in_=result[:])
 
+        gram_banks = {0: gram(0)}
         dists = {}
         pfTs = {}
         acc = {}
         for s in range(STEPS + LAG):
             done = s - LAG
-            if done == 0:
-                quantise_members()
             if done >= 0:
                 force = multiply(dists[done], pfTs[done])
             if s + 1 < STEPS:
                 gram_banks[s + 1] = gram(s + 1)
             if s < STEPS:
-                neg_half_d2 = add_norms(s, gram_banks[s])
+                dists[s] = clamp_and_root(s, gram_banks[s])
+            if 0 <= done < PASSES:
+                quantise_members(done)
             if done >= 0:
                 codes, scales = quantise(force)
             if s < STEPS:
-                dists[s] = clamp_and_root(neg_half_d2)
                 pfTs[s] = transpose_pf(s)
             if done >= 0:
                 multiply_members(done, codes, scales, acc)

@@ -39,10 +39,10 @@ FLOPS = 2 * NODES * NODES * CODE + 2 * NODES * NODES * CLUSTERS
 def tile_controencodnet_pb_kernel(tc, feats, pf_offdiag, members, out):
     nc = tc.nc
 
-    feats_nodes = feats.rearrange("(g p t) c -> p g t c", g=PASSES, t=PACK)
-    pf_rows = pf_offdiag.rearrange("(g p t) j -> p g t j", g=PASSES, t=PACK)
-    members_nodes = members.rearrange("(g p t) c -> p g t c", g=PASSES, t=PACK)
-    out_rows = out.rearrange("(g p t) c -> p g t c", g=PASSES, t=PACK)
+    feats_nodes = feats.rearrange("(g w p e) c -> p g w e c", g=PASSES, w=WORDS, e=PAIR)
+    pf_rows = pf_offdiag.rearrange("(g w p e) j -> p g w e j", g=PASSES, w=WORDS, e=PAIR)
+    members_nodes = members.rearrange("(g w p e) c -> p g w e c", g=PASSES, w=WORDS, e=PAIR)
+    out_rows = out.rearrange("(g w p e) c -> p g w e c", g=PASSES, w=WORDS, e=PAIR)
 
     with ExitStack() as ctx:
         ctx.enter_context(tc.manual_schedule())
@@ -54,17 +54,20 @@ def tile_controencodnet_pb_kernel(tc, feats, pf_offdiag, members, out):
 
         feats_sb = keep.tile([P, PASSES, PACK, CODE], BF16)
         for g in range(PASSES):
-            nc.sync.dma_start(out=feats_sb[:, g], in_=feats_nodes[:, g])
+            nc.sync.dma_start(
+                out=feats_sb[:, g].rearrange("p (w e) c -> p w e c", e=PAIR), in_=feats_nodes[:, g]
+            )
         members_sb = keep.tile([P, PASSES, PACK, CLUSTERS], BF16)
         for g in range(PASSES):
-            nc.sync.dma_start(out=members_sb[:, g], in_=members_nodes[:, g])
+            nc.sync.dma_start(
+                out=members_sb[:, g].rearrange("p (w e) c -> p w e c", e=PAIR),
+                in_=members_nodes[:, g],
+            )
         pf_sb = []
         for q in range(GROUPS):
-            g_row, t_row = divmod(q * GROUP_TILES, PACK)
+            g_row, w_row = divmod(q, WORDS)
             pf_group = keep.tile([P, GROUP_TILES, NODES], BF16, name="pf_group%d" % q)
-            nc.sync.dma_start(
-                out=pf_group[:], in_=pf_rows[:, g_row, t_row : t_row + GROUP_TILES, :]
-            )
+            nc.sync.dma_start(out=pf_group[:], in_=pf_rows[:, g_row, w_row])
             pf_sb.append(pf_group)
 
         one = keep.tile([P, 1], F32)
@@ -124,14 +127,6 @@ def tile_controencodnet_pb_kernel(tc, feats, pf_offdiag, members, out):
             for b in range(PACK // BANK_TILES):
                 bank = gram_psum.tile([P, BANK_TILES, GROUP], F32, tag="gram", name="gram_bank")
                 for h in range(BANK_TILES):
-                    a = g * PACK + b * BANK_TILES + h
-                    nc.tensor.matmul(
-                        out=bank[:, h, :],
-                        lhsT=featsT_m2[:, a * P : (a + 1) * P],
-                        rhs=featsT[:, q * GROUP : (q + 1) * GROUP],
-                        start=True,
-                        stop=False,
-                    )
                     for r in range(GROUP_TILES):
                         row_tile = q * GROUP_TILES + r
                         nc.tensor.matmul(
@@ -139,10 +134,20 @@ def tile_controencodnet_pb_kernel(tc, feats, pf_offdiag, members, out):
                             lhsT=sq[:, row_tile : row_tile + 1].to_broadcast([P, P]),
                             rhs=ident_f32[:],
                             is_transpose=True,
-                            start=False,
-                            stop=(r == GROUP_TILES - 1),
+                            start=(h == 0 and r == 0),
+                            stop=False,
                         )
                 banks.append(bank)
+            for b in range(PACK // BANK_TILES):
+                for h in range(BANK_TILES):
+                    a = g * PACK + b * BANK_TILES + h
+                    nc.tensor.matmul(
+                        out=banks[b][:, h, :],
+                        lhsT=featsT_m2[:, a * P : (a + 1) * P],
+                        rhs=featsT[:, q * GROUP : (q + 1) * GROUP],
+                        start=False,
+                        stop=(h == BANK_TILES - 1),
+                    )
             return banks
 
         def clamp_and_root(s, banks):
@@ -170,11 +175,11 @@ def tile_controencodnet_pb_kernel(tc, feats, pf_offdiag, members, out):
             pfT = pft_psum.tile([P, WORDS * GROUP], F32, tag="pft")
             for r in range(GROUP_TILES):
                 row_words = pf_sb[q][:, r, :].bitcast(F32)
-                pass_words = K_PASS // PAIR
                 for w in range(WORDS):
+                    first_word = (g * WORDS + w) * P
                     nc.tensor.transpose(
                         pfT[:, w * GROUP + r * P : w * GROUP + (r + 1) * P],
-                        row_words[:, g * pass_words + w : (g + 1) * pass_words : WORDS],
+                        row_words[:, first_word : first_word + P],
                         ident_f32[:],
                     )
             return pfT
@@ -211,10 +216,10 @@ def tile_controencodnet_pb_kernel(tc, feats, pf_offdiag, members, out):
                 )
             if g == PASSES - 1:
                 for r in range(GROUP_TILES):
-                    g_row, t_row = divmod(q * GROUP_TILES + r, PACK)
+                    g_row, w_row = divmod(q, WORDS)
                     result = work.tile([P, CLUSTERS], F32, tag="result")
                     nc.scalar.copy(out=result[:], in_=acc[r][:])
-                    nc.sync.dma_start(out=out_rows[:, g_row, t_row, :], in_=result[:])
+                    nc.sync.dma_start(out=out_rows[:, g_row, w_row, r, :], in_=result[:])
 
         gram_banks = {0: gram(0)}
         dists = {}

@@ -225,19 +225,21 @@ def tile_controencodnet_pb_kernel(tc, feats, pf_offdiag, members, out):
         dists = {}
         pfTs = {}
         acc = {}
-        for s in range(STEPS + LAG):
-            done = s - LAG
-            if done >= 0:
-                force = multiply(dists[done], pfTs[done])
+        quantised = {}
+        for s in range(STEPS + LAG + 1):
+            rooted = s - LAG
+            if 0 <= rooted - 1:
+                codes, scales = quantised[rooted - 1]
+                multiply_members(rooted - 1, codes, scales, acc)
+            if 0 <= rooted < STEPS:
+                force = multiply(dists[rooted], pfTs[rooted])
+            if 0 <= s - 1 < STEPS:
+                pfTs[s - 1] = transpose_pf(s - 1)
             if s + 1 < STEPS:
                 gram_banks[s + 1] = gram(s + 1)
             if s < STEPS:
                 dists[s] = clamp_and_root(s, gram_banks[s])
-            if 0 <= done < PASSES:
-                quantise_members(done)
-            if done >= 0:
-                codes, scales = quantise(force)
-            if s < STEPS:
-                pfTs[s] = transpose_pf(s)
-            if done >= 0:
-                multiply_members(done, codes, scales, acc)
+            if 0 <= rooted < PASSES:
+                quantise_members(rooted)
+            if 0 <= rooted < STEPS:
+                quantised[rooted] = quantise(force)

@@ -39,10 +39,10 @@ FLOPS = 2 * NODES * NODES * CODE + 2 * NODES * NODES * CLUSTERS
 def tile_controencodnet_pb_kernel(tc, feats, pf_offdiag, members, out):
     nc = tc.nc
 
-    feats_nodes = feats.rearrange("(g w p e) c -> p g w e c", g=PASSES, w=WORDS, e=PAIR)
-    pf_rows = pf_offdiag.rearrange("(g w p e) j -> p g w e j", g=PASSES, w=WORDS, e=PAIR)
-    members_nodes = members.rearrange("(g w p e) c -> p g w e c", g=PASSES, w=WORDS, e=PAIR)
-    out_rows = out.rearrange("(g w p e) c -> p g w e c", g=PASSES, w=WORDS, e=PAIR)
+    feats_nodes = feats.rearrange("(g p t) c -> p g t c", g=PASSES, t=PACK)
+    pf_rows = pf_offdiag.rearrange("(g p t) j -> p g t j", g=PASSES, t=PACK)
+    members_nodes = members.rearrange("(g p t) c -> p g t c", g=PASSES, t=PACK)
+    out_rows = out.rearrange("(g p t) c -> p g t c", g=PASSES, t=PACK)
 
     with ExitStack() as ctx:
         ctx.enter_context(tc.manual_schedule())
@@ -54,20 +54,17 @@ def tile_controencodnet_pb_kernel(tc, feats, pf_offdiag, members, out):
 
         feats_sb = keep.tile([P, PASSES, PACK, CODE], BF16)
         for g in range(PASSES):
-            nc.sync.dma_start(
-                out=feats_sb[:, g].rearrange("p (w e) c -> p w e c", e=PAIR), in_=feats_nodes[:, g]
-            )
+            nc.sync.dma_start(out=feats_sb[:, g], in_=feats_nodes[:, g])
         members_sb = keep.tile([P, PASSES, PACK, CLUSTERS], BF16)
         for g in range(PASSES):
-            nc.sync.dma_start(
-                out=members_sb[:, g].rearrange("p (w e) c -> p w e c", e=PAIR),
-                in_=members_nodes[:, g],
-            )
+            nc.sync.dma_start(out=members_sb[:, g], in_=members_nodes[:, g])
         pf_sb = []
         for q in range(GROUPS):
-            g_row, w_row = divmod(q, WORDS)
+            g_row, t_row = divmod(q * GROUP_TILES, PACK)
             pf_group = keep.tile([P, GROUP_TILES, NODES], BF16, name="pf_group%d" % q)
-            nc.sync.dma_start(out=pf_group[:], in_=pf_rows[:, g_row, w_row])
+            nc.sync.dma_start(
+                out=pf_group[:], in_=pf_rows[:, g_row, t_row : t_row + GROUP_TILES, :]
+            )
             pf_sb.append(pf_group)
 
         one = keep.tile([P, 1], F32)
@@ -175,11 +172,11 @@ def tile_controencodnet_pb_kernel(tc, feats, pf_offdiag, members, out):
             pfT = pft_psum.tile([P, WORDS * GROUP], F32, tag="pft")
             for r in range(GROUP_TILES):
                 row_words = pf_sb[q][:, r, :].bitcast(F32)
+                pass_words = K_PASS // PAIR
                 for w in range(WORDS):
-                    first_word = (g * WORDS + w) * P
                     nc.tensor.transpose(
                         pfT[:, w * GROUP + r * P : w * GROUP + (r + 1) * P],
-                        row_words[:, first_word : first_word + P],
+                        row_words[:, g * pass_words + w : (g + 1) * pass_words : WORDS],
                         ident_f32[:],
                     )
             return pfT
@@ -216,30 +213,28 @@ def tile_controencodnet_pb_kernel(tc, feats, pf_offdiag, members, out):
                 )
             if g == PASSES - 1:
                 for r in range(GROUP_TILES):
-                    g_row, w_row = divmod(q, WORDS)
+                    g_row, t_row = divmod(q * GROUP_TILES + r, PACK)
                     result = work.tile([P, CLUSTERS], F32, tag="result")
                     nc.scalar.copy(out=result[:], in_=acc[r][:])
-                    nc.sync.dma_start(out=out_rows[:, g_row, w_row, r, :], in_=result[:])
+                    nc.sync.dma_start(out=out_rows[:, g_row, t_row, :], in_=result[:])
 
         gram_banks = {0: gram(0)}
         dists = {}
         pfTs = {}
         acc = {}
-        quantised = {}
-        for s in range(STEPS + LAG + 1):
-            rooted = s - LAG
-            if 0 <= rooted - 1:
-                codes, scales = quantised[rooted - 1]
-                multiply_members(rooted - 1, codes, scales, acc)
-            if 0 <= rooted < STEPS:
-                force = multiply(dists[rooted], pfTs[rooted])
-            if 0 <= s - 1 < STEPS:
-                pfTs[s - 1] = transpose_pf(s - 1)
+        for s in range(STEPS + LAG):
+            done = s - LAG
+            if done >= 0:
+                force = multiply(dists[done], pfTs[done])
             if s + 1 < STEPS:
                 gram_banks[s + 1] = gram(s + 1)
             if s < STEPS:
                 dists[s] = clamp_and_root(s, gram_banks[s])
-            if 0 <= rooted < PASSES:
-                quantise_members(rooted)
-            if 0 <= rooted < STEPS:
-                quantised[rooted] = quantise(force)
+            if 0 <= done < PASSES:
+                quantise_members(done)
+            if done >= 0:
+                codes, scales = quantise(force)
+            if s < STEPS:
+                pfTs[s] = transpose_pf(s)
+            if done >= 0:
+                multiply_members(done, codes, scales, acc)

from contextlib import ExitStack

import concourse.mybir as mybir
from concourse.masks import make_identity

F32 = mybir.dt.float32
BF16 = mybir.dt.bfloat16
U32 = mybir.dt.uint32
U8 = mybir.dt.uint8
FP8X4 = mybir.dt.float8_e4m3fn_x4
ALU = mybir.AluOpType
ACT = mybir.ActivationFunctionType

NODES = 1024
CODE = 128
CLUSTERS = 512
D2_FLOOR = 1e-12

P = 128
PACK = 4
K_PASS = P * PACK
PASSES = NODES // K_PASS
TILES = NODES // P
BANK = 512

GROUP_TILES = 2
GROUP = GROUP_TILES * P
GROUPS = NODES // GROUP
STEPS = GROUPS * PASSES
BANK_TILES = BANK // GROUP
PAIR = 2
WORDS = PACK // PAIR

LAG = 2

FLOPS = 2 * NODES * NODES * CODE + 2 * NODES * NODES * CLUSTERS


def tile_controencodnet_pb_kernel(tc, feats, pf_offdiag, members, out):
    nc = tc.nc

    feats_nodes = feats.rearrange("(g p t) c -> p g t c", g=PASSES, t=PACK)
    pf_rows = pf_offdiag.rearrange("(g p t) j -> p g t j", g=PASSES, t=PACK)
    members_nodes = members.rearrange("(g p t) c -> p g t c", g=PASSES, t=PACK)
    out_rows = out.rearrange("(g p t) c -> p g t c", g=PASSES, t=PACK)

    with ExitStack() as ctx:
        ctx.enter_context(tc.manual_schedule())
        keep = ctx.enter_context(tc.tile_pool(name="keep", bufs=1))
        work = ctx.enter_context(tc.tile_pool(name="work", bufs=LAG + 1))
        gram_psum = ctx.enter_context(tc.psum_pool(name="gram_psum", bufs=4))
        pft_psum = ctx.enter_context(tc.psum_pool(name="pft_psum", bufs=2))
        acc_psum = ctx.enter_context(tc.psum_pool(name="acc_psum", bufs=GROUP_TILES))

        feats_sb = keep.tile([P, PASSES, PACK, CODE], BF16)
        for g in range(PASSES):
            nc.sync.dma_start(out=feats_sb[:, g], in_=feats_nodes[:, g])
        members_sb = keep.tile([P, PASSES, PACK, CLUSTERS], BF16)
        for g in range(PASSES):
            nc.sync.dma_start(out=members_sb[:, g], in_=members_nodes[:, g])
        pf_sb = []
        for q in range(GROUPS):
            g_row, t_row = divmod(q * GROUP_TILES, PACK)
            pf_group = keep.tile([P, GROUP_TILES, NODES], BF16, name="pf_group%d" % q)
            nc.sync.dma_start(
                out=pf_group[:], in_=pf_rows[:, g_row, t_row : t_row + GROUP_TILES, :]
            )
            pf_sb.append(pf_group)

        one = keep.tile([P, 1], F32)
        nc.vector.memset(one[:], 1.0)
        nc.scalar.activation(out=one[:], in_=one[:], func=ACT.Sqrt)
        ident_bf16 = keep.tile([P, P], BF16)
        make_identity(nc, ident_bf16[:])
        ident_f32 = keep.tile([P, P], F32)
        make_identity(nc, ident_f32[:])

        featsT = keep.tile([P, NODES], BF16)
        featsT_m2 = keep.tile([P, NODES], BF16)
        for g in range(PASSES):
            featsT_ps = pft_psum.tile([P, K_PASS], BF16, tag="pft")
            for t in range(PACK):
                nc.tensor.transpose(
                    featsT_ps[:, t * P : (t + 1) * P], feats_sb[:, g, t, :], ident_bf16[:]
                )
            pass_cols = slice(g * K_PASS, (g + 1) * K_PASS)
            nc.vector.tensor_copy(out=featsT[:, pass_cols], in_=featsT_ps[:])
            nc.vector.tensor_scalar_mul(out=featsT_m2[:, pass_cols], in0=featsT_ps[:], scalar1=-2.0)

        squares = keep.tile([P, TILES, CODE], F32)
        sq = keep.tile([P, TILES], F32)
        for a in range(TILES):
            g, t = divmod(a, PACK)
            nc.scalar.activation(
                out=squares[:, a, :],
                in_=feats_sb[:, g, t, :],
                func=ACT.Square,
                accum_out=sq[:, a : a + 1],
            )

        members_grouped = keep.tile([P, PASSES, CLUSTERS, PACK], BF16, align_bytes=64)
        for g in range(PASSES):
            nc.gpsimd.tensor_scalar(
                out=members_grouped[:, g],
                in0=members_sb[:, g].rearrange("p t c -> p c t"),
                scalar1=1.0,
                scalar2=0.0,
                op0=ALU.mult,
                op1=ALU.add,
            )
        members_codes = keep.tile([P, PASSES, CLUSTERS], U32, align_bytes=64)
        members_scales = keep.tile([P, PASSES, CLUSTERS], U8, align_bytes=64)

        def quantise_members(g):
            nc.vector.quantize_mx(
                out=members_codes[:, g, :].bitcast(FP8X4),
                scales=members_scales[:, g, :],
                in_=members_grouped[:, g].rearrange("p c t -> p (c t)"),
            )

        def gram(s):
            q, g = divmod(s, PASSES)
            banks = []
            for b in range(PACK // BANK_TILES):
                bank = gram_psum.tile([P, BANK_TILES, GROUP], F32, tag="gram", name="gram_bank")
                for h in range(BANK_TILES):
                    for r in range(GROUP_TILES):
                        row_tile = q * GROUP_TILES + r
                        nc.tensor.matmul(
                            out=bank[:, h, r * P : (r + 1) * P],
                            lhsT=sq[:, row_tile : row_tile + 1].to_broadcast([P, P]),
                            rhs=ident_f32[:],
                            is_transpose=True,
                            start=(h == 0 and r == 0),
                            stop=False,
                        )
                banks.append(bank)
            for b in range(PACK // BANK_TILES):
                for h in range(BANK_TILES):
                    a = g * PACK + b * BANK_TILES + h
                    nc.tensor.matmul(
                        out=banks[b][:, h, :],
                        lhsT=featsT_m2[:, a * P : (a + 1) * P],
                        rhs=featsT[:, q * GROUP : (q + 1) * GROUP],
                        start=False,
                        stop=(h == BANK_TILES - 1),
                    )
            return banks

        def clamp_and_root(s, banks):
            g = s % PASSES
            d2 = work.tile([P, PACK, GROUP], F32, tag="d2")
            for t in range(PACK):
                b, h = divmod(t, BANK_TILES)
                a = g * PACK + t
                nc.vector.tensor_scalar(
                    out=d2[:, t, :],
                    in0=banks[b][:, h, :],
                    scalar1=sq[:, a : a + 1],
                    scalar2=D2_FLOOR,
                    op0=ALU.add,
                    op1=ALU.max,
                )
            dist = work.tile([P, GROUP, PACK], F32, tag="dist")
            nc.scalar.activation(
                out=dist[:], in_=d2[:].rearrange("p t n -> p n t"), func=ACT.Sqrt
            )
            return dist

        def transpose_pf(s):
            q, g = divmod(s, PASSES)
            pfT = pft_psum.tile([P, WORDS * GROUP], F32, tag="pft")
            for r in range(GROUP_TILES):
                row_words = pf_sb[q][:, r, :].bitcast(F32)
                pass_words = K_PASS // PAIR
                for w in range(WORDS):
                    nc.tensor.transpose(
                        pfT[:, w * GROUP + r * P : w * GROUP + (r + 1) * P],
                        row_words[:, g * pass_words + w : (g + 1) * pass_words : WORDS],
                        ident_f32[:],
                    )
            return pfT

        def multiply(dist, pfT):
            force = work.tile([P, GROUP * PACK], BF16, tag="force", align_bytes=64)
            nc.vector.tensor_tensor(
                out=force[:].rearrange("p (n w e) -> p n w e", w=WORDS, e=PAIR),
                in0=dist[:].rearrange("p n (w e) -> p n w e", e=PAIR),
                in1=pfT[:].bitcast(BF16).rearrange("p (w n e) -> p n w e", w=WORDS, e=PAIR),
                op=ALU.mult,
            )
            return force

        def quantise(force):
            codes = work.tile([P, GROUP], U32, tag="codes", align_bytes=64)
            scales = work.tile([P, GROUP], U8, tag="scales", align_bytes=64)
            nc.vector.quantize_mx(out=codes[:].bitcast(FP8X4), scales=scales[:], in_=force[:])
            return codes, scales

        def multiply_members(s, codes, scales, acc):
            q, g = divmod(s, PASSES)
            for r in range(GROUP_TILES):
                if g == 0:
                    acc[r] = acc_psum.tile([P, CLUSTERS], F32, tag="acc", name="acc_bank")
                nc.tensor.matmul_mx(
                    out=acc[r][:],
                    lhsT=codes[:, r * P : (r + 1) * P].bitcast(FP8X4),
                    lhsT_scale=scales[:, r * P : (r + 1) * P],
                    rhs=members_codes[:, g, :].bitcast(FP8X4),
                    rhs_scale=members_scales[:, g, :],
                    start=(g == 0),
                    stop=(g == PASSES - 1),
                )
            if g == PASSES - 1:
                for r in range(GROUP_TILES):
                    g_row, t_row = divmod(q * GROUP_TILES + r, PACK)
                    result = work.tile([P, CLUSTERS], F32, tag="result")
                    nc.scalar.copy(out=result[:], in_=acc[r][:])
                    nc.sync.dma_start(out=out_rows[:, g_row, t_row, :], in_=result[:])

        gram_banks = {0: gram(0)}
        dists = {}
        pfTs = {}
        acc = {}
        for s in range(STEPS + LAG):
            done = s - LAG
            if done >= 0:
                force = multiply(dists[done], pfTs[done])
            if s + 1 < STEPS:
                gram_banks[s + 1] = gram(s + 1)
            if s < STEPS:
                dists[s] = clamp_and_root(s, gram_banks[s])
            if 0 <= done < PASSES:
                quantise_members(done)
            if done >= 0:
                codes, scales = quantise(force)
            if s < STEPS:
                pfTs[s] = transpose_pf(s)
            if done >= 0:
                multiply_members(done, codes, scales, acc)
